import numpy as np
import ml_dtypes


def mxq(x, axis, fmt="e4m3"):
    dtype, down = {"e4m3": (ml_dtypes.float8_e4m3fn, 7), "e5m2": (ml_dtypes.float8_e5m2, 14)}[fmt]
    v = np.moveaxis(np.asarray(x, np.float32).astype(ml_dtypes.bfloat16).astype(np.float64), axis, -1)
    blocks = v.reshape(v.shape[:-1] + (-1, 32))
    amax = np.abs(blocks).max(-1, keepdims=True)
    byte = np.maximum(np.where(amax > 0, np.frexp(amax)[1] - 1 + 127, 0) - down, 1)
    scale = np.exp2(byte - 127.0)
    codes = (blocks / scale).astype(np.float32).astype(dtype).astype(np.float64)
    return np.moveaxis((codes * scale).reshape(v.shape), -1, axis)


WIDE = False


def mx_kscale(k):
    if not WIDE:
        return np.ones(k)
    levels = np.array([10, -10, 5, -5, 0])
    a = np.random.permutation(np.resize(levels, k // 512 * 4)).reshape(k // 512, 4)
    idx = np.arange(k)
    return np.exp2(a[idx // 512, idx % 128 // 32])


BF16 = ml_dtypes.bfloat16


def bf(x):
    return np.asarray(x, np.float32).astype(BF16)


def f64(x):
    return np.asarray(x).astype(np.float64)


E2M1 = np.array([0.0, 0.5, 1.0, 1.5, 2.0, 3.0, 4.0, 6.0, -0.0, -0.5, -1.0, -1.5, -2.0, -3.0, -4.0, -6.0])


def pack_weight(w, fmt):
    k, n = w.shape
    w = f64(bf(w)).reshape(k // 32, 32, n)
    amax = np.abs(w).max(1)
    if fmt == "e4m3":
        byte = np.frexp(amax)[1] - 1 + 127 - 7
    else:
        mant, ex = np.frexp(amax / 6.0)
        byte = np.where(mant > 0.5, ex, ex - 1) + 127
    byte = np.clip(np.where(amax > 0, byte, 1), 1, 254)
    scaled = (w * np.exp2(127.0 - byte)[:, None, :]).reshape(k, n).astype(np.float32)
    by_word = np.ascontiguousarray(scaled.reshape(k // 512, 128, 4, n).transpose(0, 1, 3, 2))
    if fmt == "e4m3":
        words = by_word.astype(ml_dtypes.float8_e4m3fn).view(np.uint8)
    else:
        c = by_word.astype(ml_dtypes.float4_e2m1fn).view(np.uint8) & 0xF
        words = c[..., 0::2] | (c[..., 1::2] << 4)
    return np.ascontiguousarray(words), np.ascontiguousarray(byte.astype(np.uint8).reshape(k // 512, 16, n))


def unpack_weight(words, scales, fmt):
    g, p, n, _ = words.shape
    if fmt == "e4m3":
        vals = np.ascontiguousarray(words).view(ml_dtypes.float8_e4m3fn).astype(np.float64)
    else:
        nib = np.empty((g, p, n, 4), np.uint8)
        nib[..., 0::2] = words & 0xF
        nib[..., 1::2] = words >> 4
        vals = E2M1[nib]
    vals = vals * np.repeat(np.exp2(scales.astype(np.float64) - 127.0), 8, axis=1)[..., None]
    return vals.transpose(0, 1, 3, 2).reshape(g * 512, n)


B, IMG, P0, P1, C, F = 2, 512, 8, 16, 2, 512
E0, E1 = IMG // P0, IMG // P1
N0, N1 = E0 * E0, E1 * E1
D0, D1 = P0 * P0 * C, P1 * P1 * C


def setup_inputs():
    s = mx_kscale(D1)
    flat = np.random.standard_normal((B, N1, D1)) * s
    img = flat.reshape(B, E1, E1, P1, P1, C).transpose(0, 1, 3, 2, 4, 5).reshape(B, IMG, IMG, C)
    encoded = img.reshape(B, E0, P0, E0, P0, C).transpose(0, 1, 3, 2, 4, 5).reshape(B, N0, D0)
    words, scales = pack_weight(np.random.standard_normal((D1, F)) / np.sqrt(D1) / s[:, None], "e4m3")
    return {"encoded": bf(encoded),
            "W_words": words,
            "W_scales": scales,
            "b": bf(np.random.standard_normal(F) * 0.3),
            "pos_emb": bf(np.random.standard_normal((N1, F)) * 0.5)}


def reference(encoded, W_words, W_scales, b, pos_emb):
    x = f64(encoded).reshape(-1, E0, E0, P0, P0, C)
    img = x.transpose(0, 1, 3, 2, 4, 5).reshape(-1, IMG, IMG, C)
    new_patches = img.reshape(-1, E1, P1, E1, P1, C).transpose(0, 1, 3, 2, 4, 5)
    flat = new_patches.reshape(-1, N1, D1)
    return (mxq(flat, 2, "e4m3") @ unpack_weight(W_words, W_scales, "e4m3")) + f64(b) + f64(pos_emb)

@@ -1,0 +1,140 @@
+import concourse.mybir as mybir
+from concourse.masks import make_identity
+
+F32 = mybir.dt.float32
+BF16 = mybir.dt.bfloat16
+I32 = mybir.dt.int32
+U32 = mybir.dt.uint32
+U8 = mybir.dt.uint8
+FP8X4 = mybir.dt.float8_e4m3fn_x4
+ADD = mybir.AluOpType.add
+
+P = 128
+IMAGES = 2
+FEATURES = 512
+K = 512
+K_WORDS = K // 2
+TOKENS_PER_PARTITION = 8
+ROUND_TILES = 4
+HALVES = TOKENS_PER_PARTITION // ROUND_TILES
+BANK_TILES = 2
+GRID = 32
+COLUMN_GROUPS = GRID // TOKENS_PER_PARTITION
+
+FLOPS = 2 * IMAGES * GRID * GRID * K * FEATURES
+
+
+def tile_resampling_kernel(tc, encoded, W_words, W_scales, b, pos_emb, out):
+    nc = tc.nc
+
+    enc_runs = encoded.rearrange(
+        "i (y ry xq r) d -> i ry y xq (r d)", y=GRID, ry=2, xq=COLUMN_GROUPS, r=2 * TOKENS_PER_PARTITION
+    )
+    pos_rows = pos_emb.rearrange("(a t) f -> a t f", t=TOKENS_PER_PARTITION)
+    out_rows = out.rearrange("i (a t) f -> i a t f", t=TOKENS_PER_PARTITION)
+    round_run = ROUND_TILES * K // 2
+
+    with tc.tile_pool(name="const", bufs=1) as const, tc.tile_pool(name="stream", bufs=4) as stream, tc.tile_pool(
+        name="results", bufs=6
+    ) as results, tc.psum_pool(name="psum_x", bufs=4) as psum_x, tc.psum_pool(name="psum_acc", bufs=4) as psum_acc:
+        w_words = const.tile([P, 4 * FEATURES], U8, align_bytes=64)
+        w_plane = const.tile([P, FEATURES], U8, align_bytes=64)
+        ident = const.tile([P, P], F32)
+        ones = const.tile([P, P], BF16)
+        bias_row = const.tile([P, FEATURES], BF16)
+        bias_all = const.tile([P, FEATURES], F32)
+        pos_sb = const.tile([P, TOKENS_PER_PARTITION, FEATURES], BF16)
+        pos_bias = const.tile([P, TOKENS_PER_PARTITION, FEATURES], F32)
+
+        nc.vector.memset(w_plane[:].bitcast(I32), 0)
+        nc.vector.memset(ones[:], 1.0)
+        nc.gpsimd.memset(bias_row[:], 0.0)
+        nc.gpsimd.dma_start(out=bias_row[0:1, :], in_=b.rearrange("(o f) -> o f", o=1))
+        make_identity(nc, ident[:])
+        for quadrant in range(4):
+            nc.gpsimd.dma_start(
+                out=w_plane[32 * quadrant : 32 * quadrant + 4, :].bitcast(F32),
+                in_=W_scales[0][4 * quadrant : 4 * quadrant + 4, :].bitcast(F32),
+            )
+
+        def load_round(image, half):
+            raw = stream.tile([P, 2, round_run], BF16, name="raw")
+            for ry in range(2):
+                nc.sync.dma_start(
+                    out=raw[:, ry, :], in_=enc_runs[image, ry][:, :, half * round_run : (half + 1) * round_run]
+                )
+            return raw
+
+        def load_pos(half):
+            tiles = slice(half * ROUND_TILES, (half + 1) * ROUND_TILES)
+            nc.sync.dma_start(out=pos_sb[:, tiles, :], in_=pos_rows[:, tiles, :])
+
+        raws = {}
+        raws[(0, 0)] = load_round(0, 0)
+        load_pos(0)
+        nc.sync.dma_start(
+            out=w_words[:].bitcast(I32), in_=W_words[0].rearrange("p n t -> p (n t)").bitcast(I32)
+        )
+        raws[(0, 1)] = load_round(0, 1)
+        load_pos(1)
+        raws[(1, 0)] = load_round(1, 0)
+        raws[(1, 1)] = load_round(1, 1)
+
+        bias_ps = psum_acc.tile([P, FEATURES], F32, tag="acc")
+        nc.tensor.matmul(out=bias_ps[:], lhsT=ones[:], rhs=bias_row[:], start=True, stop=True)
+        nc.scalar.copy(out=bias_all[:], in_=bias_ps[:])
+
+        for t in range(TOKENS_PER_PARTITION):
+            engine = nc.vector if t < ROUND_TILES else nc.gpsimd
+            engine.tensor_tensor(out=pos_bias[:, t, :], in0=pos_sb[:, t, :], in1=bias_all[:], op=ADD)
+
+        def quantise_round(raw):
+            flat_sb = stream.tile([P, ROUND_TILES, K_WORDS], F32, name="flat_sb")
+            raw_v = raw[:].bitcast(F32).rearrange("p ry (t rx r8 w) -> p ry t rx r8 w", t=ROUND_TILES, rx=2, r8=8)
+            flat_v = flat_sb[:].rearrange("p t (ry r8 rx w) -> p t ry r8 rx w", ry=2, r8=8, rx=2)
+            for ry in range(2):
+                for rx in range(2):
+                    nc.scalar.copy(out=flat_v[:, :, ry, :, rx, :], in_=raw_v[:, ry, :, rx, :, :])
+            grouped = stream.tile([P, ROUND_TILES * P * 4], BF16, name="grouped", align_bytes=64)
+            grouped_v = grouped[:].bitcast(F32).rearrange("p (t a u) -> p t a u", t=ROUND_TILES, u=2)
+            for first in range(0, ROUND_TILES, BANK_TILES):
+                xt = psum_x.tile([P, BANK_TILES, 2, P], F32, name="xt")
+                for j in range(BANK_TILES):
+                    for u in range(2):
+                        nc.tensor.transpose(xt[:, j, u, :], flat_sb[:, first + j, u:K_WORDS:2], ident[:])
+                nc.scalar.copy(
+                    out=grouped_v[:, first : first + BANK_TILES], in_=xt[:].rearrange("p t u a -> p t a u")
+                )
+            codes = stream.tile([P, ROUND_TILES * P], U32, name="codes", align_bytes=64)
+            plane = stream.tile([P, ROUND_TILES * P], U8, name="plane", align_bytes=64)
+            nc.vector.quantize_mx(out=codes[:].bitcast(FP8X4), scales=plane[:], in_=grouped[:])
+            return codes, plane
+
+        def project_round(image, half, codes, plane):
+            for first in range(0, ROUND_TILES, 2):
+                result = results.tile([P, 2, FEATURES], F32, name="result")
+                for j in range(2):
+                    tokens = slice((first + j) * P, (first + j + 1) * P)
+                    t = half * ROUND_TILES + first + j
+                    acc = psum_acc.tile([P, FEATURES], F32, tag="acc")
+                    nc.tensor.matmul_mx(
+                        out=acc[:],
+                        lhsT=codes[:, tokens].bitcast(FP8X4),
+                        lhsT_scale=plane[:, tokens],
+                        rhs=w_words[:].bitcast(FP8X4),
+                        rhs_scale=w_plane[:],
+                        start=True,
+                        stop=True,
+                    )
+                    nc.vector.tensor_tensor(out=result[:, j, :], in0=acc[:], in1=pos_bias[:, t, :], op=ADD)
+                t0 = half * ROUND_TILES + first
+                nc.sync.dma_start(out=out_rows[image][:, t0 : t0 + 2, :], in_=result[:])
+
+        rounds = [(image, half) for image in range(IMAGES) for half in range(HALVES)]
+        quantised = {}
+        for step in range(len(rounds) + 1):
+            if step < len(rounds):
+                quantised[step] = quantise_round(raws[rounds[step]])
+            if step > 0:
+                image, half = rounds[step - 1]
+                project_round(image, half, quantised[step - 1][0], quantised[step - 1][1])

@@ -1,3 +1,5 @@
+from contextlib import ExitStack
+
 import concourse.mybir as mybir
 from concourse.masks import make_identity
 
@@ -15,9 +17,12 @@ FEATURES = 512
 K = 512
 K_WORDS = K // 2
 TOKENS_PER_PARTITION = 8
-ROUND_TILES = 4
-HALVES = TOKENS_PER_PARTITION // ROUND_TILES
-BANK_TILES = 2
+ROUND_TILES = 2
+LOAD_TILES = 4
+LOADS_PER_IMAGE = TOKENS_PER_PARTITION // LOAD_TILES
+ROUNDS_PER_LOAD = LOAD_TILES // ROUND_TILES
+ROUNDS = IMAGES * TOKENS_PER_PARTITION // ROUND_TILES
+VECTOR_POS_ROUNDS = 2
 GRID = 32
 COLUMN_GROUPS = GRID // TOKENS_PER_PARTITION
 
@@ -32,11 +37,17 @@ def tile_resampling_kernel(tc, encoded, W_words, W_scales, b, pos_emb, out):
     )
     pos_rows = pos_emb.rearrange("(a t) f -> a t f", t=TOKENS_PER_PARTITION)
     out_rows = out.rearrange("i (a t) f -> i a t f", t=TOKENS_PER_PARTITION)
-    round_run = ROUND_TILES * K // 2
+    load_run = LOAD_TILES * K // 2
 
-    with tc.tile_pool(name="const", bufs=1) as const, tc.tile_pool(name="stream", bufs=4) as stream, tc.tile_pool(
-        name="results", bufs=6
-    ) as results, tc.psum_pool(name="psum_x", bufs=4) as psum_x, tc.psum_pool(name="psum_acc", bufs=4) as psum_acc:
+    with ExitStack() as stack:
+        const = stack.enter_context(tc.tile_pool(name="const", bufs=1))
+        loaded = stack.enter_context(tc.tile_pool(name="loaded", bufs=IMAGES * LOADS_PER_IMAGE))
+        stream = stack.enter_context(tc.tile_pool(name="stream", bufs=4))
+        results = stack.enter_context(tc.tile_pool(name="results", bufs=8))
+        psum_x = stack.enter_context(tc.psum_pool(name="psum_x", bufs=4))
+        psum_acc = stack.enter_context(tc.psum_pool(name="psum_acc", bufs=4))
+        stack.enter_context(tc.manual_schedule())
+
         w_words = const.tile([P, 4 * FEATURES], U8, align_bytes=64)
         w_plane = const.tile([P, FEATURES], U8, align_bytes=64)
         ident = const.tile([P, P], F32)
@@ -46,95 +57,120 @@ def tile_resampling_kernel(tc, encoded, W_words, W_scales, b, pos_emb, out):
         pos_sb = const.tile([P, TOKENS_PER_PARTITION, FEATURES], BF16)
         pos_bias = const.tile([P, TOKENS_PER_PARTITION, FEATURES], F32)
 
+        nc.vector.memset(bias_row[:], 0.0)
         nc.vector.memset(w_plane[:].bitcast(I32), 0)
         nc.vector.memset(ones[:], 1.0)
-        nc.gpsimd.memset(bias_row[:], 0.0)
-        nc.gpsimd.dma_start(out=bias_row[0:1, :], in_=b.rearrange("(o f) -> o f", o=1))
         make_identity(nc, ident[:])
-        for quadrant in range(4):
-            nc.gpsimd.dma_start(
-                out=w_plane[32 * quadrant : 32 * quadrant + 4, :].bitcast(F32),
-                in_=W_scales[0][4 * quadrant : 4 * quadrant + 4, :].bitcast(F32),
-            )
 
-        def load_round(image, half):
-            raw = stream.tile([P, 2, round_run], BF16, name="raw")
+        def load_tokens(image, part):
+            raw = loaded.tile([P, 2, load_run], BF16, name="raw")
             for ry in range(2):
                 nc.sync.dma_start(
-                    out=raw[:, ry, :], in_=enc_runs[image, ry][:, :, half * round_run : (half + 1) * round_run]
+                    out=raw[:, ry, :], in_=enc_runs[image, ry][:, :, part * load_run : (part + 1) * load_run]
                 )
             return raw
 
-        def load_pos(half):
-            tiles = slice(half * ROUND_TILES, (half + 1) * ROUND_TILES)
+        def load_pos(part):
+            tiles = slice(part * LOAD_TILES, (part + 1) * LOAD_TILES)
             nc.sync.dma_start(out=pos_sb[:, tiles, :], in_=pos_rows[:, tiles, :])
 
-        raws = {}
-        raws[(0, 0)] = load_round(0, 0)
+        raws = [load_tokens(0, 0)]
+        nc.sync.dma_start(out=bias_row[0:1, :], in_=b.rearrange("(o f) -> o f", o=1))
         load_pos(0)
         nc.sync.dma_start(
             out=w_words[:].bitcast(I32), in_=W_words[0].rearrange("p n t -> p (n t)").bitcast(I32)
         )
-        raws[(0, 1)] = load_round(0, 1)
+        for quadrant in range(4):
+            nc.sync.dma_start(
+                out=w_plane[32 * quadrant : 32 * quadrant + 4, :].bitcast(I32),
+                in_=W_scales[0][4 * quadrant : 4 * quadrant + 4, :].bitcast(I32),
+            )
+        raws.append(load_tokens(0, 1))
         load_pos(1)
-        raws[(1, 0)] = load_round(1, 0)
-        raws[(1, 1)] = load_round(1, 1)
+        raws.append(load_tokens(1, 0))
+        raws.append(load_tokens(1, 1))
 
         bias_ps = psum_acc.tile([P, FEATURES], F32, tag="acc")
         nc.tensor.matmul(out=bias_ps[:], lhsT=ones[:], rhs=bias_row[:], start=True, stop=True)
-        nc.scalar.copy(out=bias_all[:], in_=bias_ps[:])
+        nc.vector.tensor_copy(out=bias_all[:], in_=bias_ps[:])
 
-        for t in range(TOKENS_PER_PARTITION):
-            engine = nc.vector if t < ROUND_TILES else nc.gpsimd
-            engine.tensor_tensor(out=pos_bias[:, t, :], in0=pos_sb[:, t, :], in1=bias_all[:], op=ADD)
+        def add_bias_to_pos(engine, r):
+            for t in range(r * ROUND_TILES, (r + 1) * ROUND_TILES):
+                engine.tensor_tensor(out=pos_bias[:, t, :], in0=pos_sb[:, t, :], in1=bias_all[:], op=ADD)
 
-        def quantise_round(raw):
+        for r in range(VECTOR_POS_ROUNDS, ROUNDS // IMAGES):
+            add_bias_to_pos(nc.gpsimd, r)
+
+        flat_of = {}
+        bank_of = {}
+        codes_of = {}
+        acc_of = {}
+
+        def sort_words(r):
+            first = (r % ROUNDS_PER_LOAD) * ROUND_TILES
+            raw_v = raws[r // ROUNDS_PER_LOAD][:].bitcast(F32).rearrange(
+                "p ry (t rx r8 w) -> p rx t ry r8 w", t=LOAD_TILES, rx=2, r8=8
+            )
             flat_sb = stream.tile([P, ROUND_TILES, K_WORDS], F32, name="flat_sb")
-            raw_v = raw[:].bitcast(F32).rearrange("p ry (t rx r8 w) -> p ry t rx r8 w", t=ROUND_TILES, rx=2, r8=8)
-            flat_v = flat_sb[:].rearrange("p t (ry r8 rx w) -> p t ry r8 rx w", ry=2, r8=8, rx=2)
-            for ry in range(2):
-                for rx in range(2):
-                    nc.scalar.copy(out=flat_v[:, :, ry, :, rx, :], in_=raw_v[:, ry, :, rx, :, :])
+            flat_v = flat_sb[:].rearrange("p t (ry r8 rx w) -> p rx t ry r8 w", ry=2, r8=8, rx=2)
+            for rx in range(2):
+                nc.scalar.copy(out=flat_v[:, rx], in_=raw_v[:, rx, first : first + ROUND_TILES])
+            flat_of[r] = flat_sb
+
+        def transpose_words(r):
+            xt = psum_x.tile([P, ROUND_TILES, 2, P], F32, name="xt")
+            for j in range(ROUND_TILES):
+                for u in range(2):
+                    nc.tensor.transpose(xt[:, j, u, :], flat_of[r][:, j, u:K_WORDS:2], ident[:])
+            bank_of[r] = xt
+
+        def quantise(r):
             grouped = stream.tile([P, ROUND_TILES * P * 4], BF16, name="grouped", align_bytes=64)
             grouped_v = grouped[:].bitcast(F32).rearrange("p (t a u) -> p t a u", t=ROUND_TILES, u=2)
-            for first in range(0, ROUND_TILES, BANK_TILES):
-                xt = psum_x.tile([P, BANK_TILES, 2, P], F32, name="xt")
-                for j in range(BANK_TILES):
-                    for u in range(2):
-                        nc.tensor.transpose(xt[:, j, u, :], flat_sb[:, first + j, u:K_WORDS:2], ident[:])
-                nc.scalar.copy(
-                    out=grouped_v[:, first : first + BANK_TILES], in_=xt[:].rearrange("p t u a -> p t a u")
-                )
+            nc.scalar.copy(out=grouped_v, in_=bank_of[r][:].rearrange("p t u a -> p t a u"))
             codes = stream.tile([P, ROUND_TILES * P], U32, name="codes", align_bytes=64)
             plane = stream.tile([P, ROUND_TILES * P], U8, name="plane", align_bytes=64)
             nc.vector.quantize_mx(out=codes[:].bitcast(FP8X4), scales=plane[:], in_=grouped[:])
-            return codes, plane
+            codes_of[r] = (codes, plane)
 
-        def project_round(image, half, codes, plane):
-            for first in range(0, ROUND_TILES, 2):
-                result = results.tile([P, 2, FEATURES], F32, name="result")
-                for j in range(2):
-                    tokens = slice((first + j) * P, (first + j + 1) * P)
-                    t = half * ROUND_TILES + first + j
-                    acc = psum_acc.tile([P, FEATURES], F32, tag="acc")
-                    nc.tensor.matmul_mx(
-                        out=acc[:],
-                        lhsT=codes[:, tokens].bitcast(FP8X4),
-                        lhsT_scale=plane[:, tokens],
-                        rhs=w_words[:].bitcast(FP8X4),
-                        rhs_scale=w_plane[:],
-                        start=True,
-                        stop=True,
-                    )
-                    nc.vector.tensor_tensor(out=result[:, j, :], in0=acc[:], in1=pos_bias[:, t, :], op=ADD)
-                t0 = half * ROUND_TILES + first
-                nc.sync.dma_start(out=out_rows[image][:, t0 : t0 + 2, :], in_=result[:])
+        def project(r):
+            codes, plane = codes_of[r]
+            acc_of[r] = []
+            for j in range(ROUND_TILES):
+                tokens = slice(j * P, (j + 1) * P)
+                acc = psum_acc.tile([P, FEATURES], F32, tag="acc")
+                nc.tensor.matmul_mx(
+                    out=acc[:],
+                    lhsT=codes[:, tokens].bitcast(FP8X4),
+                    lhsT_scale=plane[:, tokens],
+                    rhs=w_words[:].bitcast(FP8X4),
+                    rhs_scale=w_plane[:],
+                    start=True,
+                    stop=True,
+                )
+                acc_of[r].append(acc)
 
-        rounds = [(image, half) for image in range(IMAGES) for half in range(HALVES)]
-        quantised = {}
-        for step in range(len(rounds) + 1):
-            if step < len(rounds):
-                quantised[step] = quantise_round(raws[rounds[step]])
-            if step > 0:
-                image, half = rounds[step - 1]
-                project_round(image, half, quantised[step - 1][0], quantised[step - 1][1])
+        def add_and_store(r):
+            image = r * ROUND_TILES // TOKENS_PER_PARTITION
+            first = r * ROUND_TILES % TOKENS_PER_PARTITION
+            for j in range(ROUND_TILES):
+                result = results.tile([P, FEATURES], F32, name="result")
+                nc.vector.tensor_tensor(out=result[:], in0=acc_of[r][j][:], in1=pos_bias[:, first + j, :], op=ADD)
+                nc.sync.dma_start(out=out_rows[image][:, first + j, :], in_=result[:])
+
+        sort_words(0)
+        transpose_words(0)
+        sort_words(1)
+        add_bias_to_pos(nc.vector, 0)
+        for r in range(ROUNDS):
+            if r + 1 < ROUNDS:
+                transpose_words(r + 1)
+            quantise(r)
+            if r + 2 < ROUNDS:
+                sort_words(r + 2)
+            if r + 1 < VECTOR_POS_ROUNDS:
+                add_bias_to_pos(nc.vector, r + 1)
+            if r > 0:
+                add_and_store(r - 1)
+            project(r)
+        add_and_store(ROUNDS - 1)

@@ -52,6 +52,7 @@ def tile_resampling_kernel(tc, encoded, W_words, W_scales, b, pos_emb, out):
         w_plane = const.tile([P, FEATURES], U8, align_bytes=64)
         ident = const.tile([P, P], F32)
         ones = const.tile([P, P], BF16)
+        table_warmer = const.tile([P, 1], BF16)
         bias_row = const.tile([P, FEATURES], BF16)
         bias_all = const.tile([P, FEATURES], F32)
         pos_sb = const.tile([P, TOKENS_PER_PARTITION, FEATURES], BF16)
@@ -60,6 +61,7 @@ def tile_resampling_kernel(tc, encoded, W_words, W_scales, b, pos_emb, out):
         nc.vector.memset(bias_row[:], 0.0)
         nc.vector.memset(w_plane[:].bitcast(I32), 0)
         nc.vector.memset(ones[:], 1.0)
+        nc.scalar.copy(out=table_warmer[:], in_=ones[:, 0:1])
         make_identity(nc, ident[:])
 
         def load_tokens(image, part):
@@ -77,6 +79,7 @@ def tile_resampling_kernel(tc, encoded, W_words, W_scales, b, pos_emb, out):
         raws = [load_tokens(0, 0)]
         nc.sync.dma_start(out=bias_row[0:1, :], in_=b.rearrange("(o f) -> o f", o=1))
         load_pos(0)
+        raws.append(load_tokens(0, 1))
         nc.sync.dma_start(
             out=w_words[:].bitcast(I32), in_=W_words[0].rearrange("p n t -> p (n t)").bitcast(I32)
         )
@@ -85,7 +88,6 @@ def tile_resampling_kernel(tc, encoded, W_words, W_scales, b, pos_emb, out):
                 out=w_plane[32 * quadrant : 32 * quadrant + 4, :].bitcast(I32),
                 in_=W_scales[0][4 * quadrant : 4 * quadrant + 4, :].bitcast(I32),
             )
-        raws.append(load_tokens(0, 1))
         load_pos(1)
         raws.append(load_tokens(1, 0))
         raws.append(load_tokens(1, 1))

@@ -163,13 +163,13 @@ def tile_resampling_kernel(tc, encoded, W_words, W_scales, b, pos_emb, out):
         sort_words(0)
         transpose_words(0)
         sort_words(1)
+        transpose_words(1)
         add_bias_to_pos(nc.vector, 0)
         for r in range(ROUNDS):
-            if r + 1 < ROUNDS:
-                transpose_words(r + 1)
             quantise(r)
             if r + 2 < ROUNDS:
                 sort_words(r + 2)
+                transpose_words(r + 2)
             if r + 1 < VECTOR_POS_ROUNDS:
                 add_bias_to_pos(nc.vector, r + 1)
             if r > 0:

@@ -164,14 +164,13 @@ def tile_resampling_kernel(tc, encoded, W_words, W_scales, b, pos_emb, out):
         transpose_words(0)
         sort_words(1)
         transpose_words(1)
-        add_bias_to_pos(nc.vector, 0)
+        for early in range(VECTOR_POS_ROUNDS):
+            add_bias_to_pos(nc.vector, early)
         for r in range(ROUNDS):
             quantise(r)
             if r + 2 < ROUNDS:
                 sort_words(r + 2)
                 transpose_words(r + 2)
-            if r + 1 < VECTOR_POS_ROUNDS:
-                add_bias_to_pos(nc.vector, r + 1)
             if r > 0:
                 add_and_store(r - 1)
             project(r)

from contextlib import ExitStack

import concourse.mybir as mybir
from concourse.masks import make_identity

F32 = mybir.dt.float32
BF16 = mybir.dt.bfloat16
I32 = mybir.dt.int32
U32 = mybir.dt.uint32
U8 = mybir.dt.uint8
FP8X4 = mybir.dt.float8_e4m3fn_x4
ADD = mybir.AluOpType.add

P = 128
IMAGES = 2
FEATURES = 512
K = 512
K_WORDS = K // 2
TOKENS_PER_PARTITION = 8
ROUND_TILES = 2
LOAD_TILES = 4
LOADS_PER_IMAGE = TOKENS_PER_PARTITION // LOAD_TILES
ROUNDS_PER_LOAD = LOAD_TILES // ROUND_TILES
ROUNDS = IMAGES * TOKENS_PER_PARTITION // ROUND_TILES
VECTOR_POS_ROUNDS = 2
GRID = 32
COLUMN_GROUPS = GRID // TOKENS_PER_PARTITION

FLOPS = 2 * IMAGES * GRID * GRID * K * FEATURES


def tile_resampling_kernel(tc, encoded, W_words, W_scales, b, pos_emb, out):
    nc = tc.nc

    enc_runs = encoded.rearrange(
        "i (y ry xq r) d -> i ry y xq (r d)", y=GRID, ry=2, xq=COLUMN_GROUPS, r=2 * TOKENS_PER_PARTITION
    )
    pos_rows = pos_emb.rearrange("(a t) f -> a t f", t=TOKENS_PER_PARTITION)
    out_rows = out.rearrange("i (a t) f -> i a t f", t=TOKENS_PER_PARTITION)
    load_run = LOAD_TILES * K // 2

    with ExitStack() as stack:
        const = stack.enter_context(tc.tile_pool(name="const", bufs=1))
        loaded = stack.enter_context(tc.tile_pool(name="loaded", bufs=IMAGES * LOADS_PER_IMAGE))
        stream = stack.enter_context(tc.tile_pool(name="stream", bufs=4))
        results = stack.enter_context(tc.tile_pool(name="results", bufs=8))
        psum_x = stack.enter_context(tc.psum_pool(name="psum_x", bufs=4))
        psum_acc = stack.enter_context(tc.psum_pool(name="psum_acc", bufs=4))
        stack.enter_context(tc.manual_schedule())

        w_words = const.tile([P, 4 * FEATURES], U8, align_bytes=64)
        w_plane = const.tile([P, FEATURES], U8, align_bytes=64)
        ident = const.tile([P, P], F32)
        ones = const.tile([P, P], BF16)
        table_warmer = const.tile([P, 1], BF16)
        bias_row = const.tile([P, FEATURES], BF16)
        bias_all = const.tile([P, FEATURES], F32)
        pos_sb = const.tile([P, TOKENS_PER_PARTITION, FEATURES], BF16)
        pos_bias = const.tile([P, TOKENS_PER_PARTITION, FEATURES], F32)

        nc.vector.memset(bias_row[:], 0.0)
        nc.vector.memset(w_plane[:].bitcast(I32), 0)
        nc.vector.memset(ones[:], 1.0)
        nc.scalar.copy(out=table_warmer[:], in_=ones[:, 0:1])
        make_identity(nc, ident[:])

        def load_tokens(image, part):
            raw = loaded.tile([P, 2, load_run], BF16, name="raw")
            for ry in range(2):
                nc.sync.dma_start(
                    out=raw[:, ry, :], in_=enc_runs[image, ry][:, :, part * load_run : (part + 1) * load_run]
                )
            return raw

        def load_pos(part):
            tiles = slice(part * LOAD_TILES, (part + 1) * LOAD_TILES)
            nc.sync.dma_start(out=pos_sb[:, tiles, :], in_=pos_rows[:, tiles, :])

        raws = [load_tokens(0, 0)]
        nc.sync.dma_start(out=bias_row[0:1, :], in_=b.rearrange("(o f) -> o f", o=1))
        load_pos(0)
        raws.append(load_tokens(0, 1))
        nc.sync.dma_start(
            out=w_words[:].bitcast(I32), in_=W_words[0].rearrange("p n t -> p (n t)").bitcast(I32)
        )
        for quadrant in range(4):
            nc.sync.dma_start(
                out=w_plane[32 * quadrant : 32 * quadrant + 4, :].bitcast(I32),
                in_=W_scales[0][4 * quadrant : 4 * quadrant + 4, :].bitcast(I32),
            )
        load_pos(1)
        raws.append(load_tokens(1, 0))
        raws.append(load_tokens(1, 1))

        bias_ps = psum_acc.tile([P, FEATURES], F32, tag="acc")
        nc.tensor.matmul(out=bias_ps[:], lhsT=ones[:], rhs=bias_row[:], start=True, stop=True)
        nc.vector.tensor_copy(out=bias_all[:], in_=bias_ps[:])

        def add_bias_to_pos(engine, r):
            for t in range(r * ROUND_TILES, (r + 1) * ROUND_TILES):
                engine.tensor_tensor(out=pos_bias[:, t, :], in0=pos_sb[:, t, :], in1=bias_all[:], op=ADD)

        for r in range(VECTOR_POS_ROUNDS, ROUNDS // IMAGES):
            add_bias_to_pos(nc.gpsimd, r)

        flat_of = {}
        bank_of = {}
        codes_of = {}
        acc_of = {}

        def sort_words(r):
            first = (r % ROUNDS_PER_LOAD) * ROUND_TILES
            raw_v = raws[r // ROUNDS_PER_LOAD][:].bitcast(F32).rearrange(
                "p ry (t rx r8 w) -> p rx t ry r8 w", t=LOAD_TILES, rx=2, r8=8
            )
            flat_sb = stream.tile([P, ROUND_TILES, K_WORDS], F32, name="flat_sb")
            flat_v = flat_sb[:].rearrange("p t (ry r8 rx w) -> p rx t ry r8 w", ry=2, r8=8, rx=2)
            for rx in range(2):
                nc.scalar.copy(out=flat_v[:, rx], in_=raw_v[:, rx, first : first + ROUND_TILES])
            flat_of[r] = flat_sb

        def transpose_words(r):
            xt = psum_x.tile([P, ROUND_TILES, 2, P], F32, name="xt")
            for j in range(ROUND_TILES):
                for u in range(2):
                    nc.tensor.transpose(xt[:, j, u, :], flat_of[r][:, j, u:K_WORDS:2], ident[:])
            bank_of[r] = xt

        def quantise(r):
            grouped = stream.tile([P, ROUND_TILES * P * 4], BF16, name="grouped", align_bytes=64)
            grouped_v = grouped[:].bitcast(F32).rearrange("p (t a u) -> p t a u", t=ROUND_TILES, u=2)
            nc.scalar.copy(out=grouped_v, in_=bank_of[r][:].rearrange("p t u a -> p t a u"))
            codes = stream.tile([P, ROUND_TILES * P], U32, name="codes", align_bytes=64)
            plane = stream.tile([P, ROUND_TILES * P], U8, name="plane", align_bytes=64)
            nc.vector.quantize_mx(out=codes[:].bitcast(FP8X4), scales=plane[:], in_=grouped[:])
            codes_of[r] = (codes, plane)

        def project(r):
            codes, plane = codes_of[r]
            acc_of[r] = []
            for j in range(ROUND_TILES):
                tokens = slice(j * P, (j + 1) * P)
                acc = psum_acc.tile([P, FEATURES], F32, tag="acc")
                nc.tensor.matmul_mx(
                    out=acc[:],
                    lhsT=codes[:, tokens].bitcast(FP8X4),
                    lhsT_scale=plane[:, tokens],
                    rhs=w_words[:].bitcast(FP8X4),
                    rhs_scale=w_plane[:],
                    start=True,
                    stop=True,
                )
                acc_of[r].append(acc)

        def add_and_store(r):
            image = r * ROUND_TILES // TOKENS_PER_PARTITION
            first = r * ROUND_TILES % TOKENS_PER_PARTITION
            for j in range(ROUND_TILES):
                result = results.tile([P, FEATURES], F32, name="result")
                nc.vector.tensor_tensor(out=result[:], in0=acc_of[r][j][:], in1=pos_bias[:, first + j, :], op=ADD)
                nc.sync.dma_start(out=out_rows[image][:, first + j, :], in_=result[:])

        sort_words(0)
        transpose_words(0)
        sort_words(1)
        transpose_words(1)
        for early in range(VECTOR_POS_ROUNDS):
            add_bias_to_pos(nc.vector, early)
        for r in range(ROUNDS):
            quantise(r)
            if r + 2 < ROUNDS:
                sort_words(r + 2)
                transpose_words(r + 2)
            if r > 0:
                add_and_store(r - 1)
            project(r)
        add_and_store(ROUNDS - 1)
